import numpy as np
import ml_dtypes


def mxq(x, axis, fmt="e4m3"):
    dtype, down = {"e4m3": (ml_dtypes.float8_e4m3fn, 7), "e5m2": (ml_dtypes.float8_e5m2, 14)}[fmt]
    v = np.moveaxis(np.asarray(x, np.float32).astype(ml_dtypes.bfloat16).astype(np.float64), axis, -1)
    blocks = v.reshape(v.shape[:-1] + (-1, 32))
    amax = np.abs(blocks).max(-1, keepdims=True)
    byte = np.maximum(np.where(amax > 0, np.frexp(amax)[1] - 1 + 127, 0) - down, 1)
    scale = np.exp2(byte - 127.0)
    codes = (blocks / scale).astype(np.float32).astype(dtype).astype(np.float64)
    return np.moveaxis((codes * scale).reshape(v.shape), -1, axis)


WIDE = False


def mx_kscale(k):
    if not WIDE:
        return np.ones(k)
    levels = np.array([10, -10, 5, -5, 0])
    a = np.random.permutation(np.resize(levels, k // 512 * 4)).reshape(k // 512, 4)
    idx = np.arange(k)
    return np.exp2(a[idx // 512, idx % 128 // 32])


BF16 = ml_dtypes.bfloat16


def bf(x):
    return np.asarray(x, np.float32).astype(BF16)


def f64(x):
    return np.asarray(x).astype(np.float64)


B, N, D, LAYER_NUM = 2, 64, 512, 2


def setup_inputs():
    fin = mx_kscale(D)
    user = bf(np.random.standard_normal((B, N, D)) * fin)
    parts = []
    for l in range(LAYER_NUM):
        fout = mx_kscale(D) if l + 1 < LAYER_NUM else np.ones(D)
        parts.append((np.random.standard_normal((B, D, D)) * 1.2 / np.sqrt(D) / fin[:, None] * fout).reshape(B, D * D))
        parts.append(np.random.standard_normal((B, D)) * 0.5 * fout)
        fin = fout
    return {"user_emb": user, "item_emb": bf(np.concatenate(parts, axis=1))}


def reference(user_emb, item_emb):
    x = f64(user_emb)
    item = f64(item_emb)
    nb = x.shape[0]
    off = 0
    for _ in range(LAYER_NUM):
        W = item[:, off:off + D * D].reshape(nb, D, D)
        off += D * D
        b = item[:, off:off + D].reshape(nb, 1, D)
        off += D
        x = np.maximum((mxq(x, 2, "e4m3") @ mxq(W, 1, "e4m3")) + b, 0.0)
    return x

@@ -1,0 +1,132 @@
+from contextlib import ExitStack
+
+import concourse.mybir as mybir
+from concourse.masks import make_identity
+
+F32 = mybir.dt.float32
+BF16 = mybir.dt.bfloat16
+U32 = mybir.dt.uint32
+U8 = mybir.dt.uint8
+FP8X4 = mybir.dt.float8_e4m3fn_x4
+ADD = mybir.AluOpType.add
+RELU = mybir.ActivationFunctionType.Relu
+
+P = 128
+PACK = 4
+D = P * PACK
+SAMPLES = 2
+ROWS = 64
+ALL_ROWS = SAMPLES * ROWS
+LAYERS = 2
+VECTOR_BLOCKS = 2
+
+FLOPS = 2 * SAMPLES * LAYERS * ROWS * D * D
+
+
+def quantise_weights(nc, raw, grouped, codes, scales):
+    source = raw[:].rearrange("p t (m j) -> p m t j", j=PACK)
+    target = grouped[:].rearrange("p j m t -> p m t j")
+    nc.vector.tensor_copy(out=target[:, :, :, :VECTOR_BLOCKS], in_=source[:, :, :, :VECTOR_BLOCKS])
+    nc.scalar.copy(out=target[:, :, :, VECTOR_BLOCKS:], in_=source[:, :, :, VECTOR_BLOCKS:])
+    for blocks in (slice(0, VECTOR_BLOCKS), slice(VECTOR_BLOCKS, PACK)):
+        nc.vector.quantize_mx(
+            out=codes[:, blocks, :].rearrange("p j m -> p (j m)").bitcast(FP8X4),
+            scales=scales[:, blocks, :].rearrange("p j m -> p (j m)"),
+            in_=grouped[:, blocks, :, :].rearrange("p j m t -> p (j m t)"),
+        )
+
+
+def multiply(nc, acc, codes, scales, act_codes, act_scales):
+    for j in range(PACK):
+        nc.tensor.matmul_mx(
+            out=acc[:, j, :],
+            lhsT=codes[:, j, :].bitcast(FP8X4),
+            lhsT_scale=scales[:, j, :],
+            rhs=act_codes[:].bitcast(FP8X4),
+            rhs_scale=act_scales[:],
+            start=True,
+            stop=True,
+        )
+
+
+def tile_can_s_kernel(tc, user_emb, item_emb, out):
+    nc = tc.nc
+    params = item_emb.rearrange("b (l r) -> (b l) r", l=LAYERS)
+
+    with ExitStack() as ctx:
+        keep = ctx.enter_context(tc.tile_pool(name="keep", bufs=1))
+        psum = ctx.enter_context(tc.psum_pool(name="psum", bufs=1))
+
+        x_rows = keep.tile([ALL_ROWS, D], BF16)
+        nc.sync.dma_start(out=x_rows[:], in_=user_emb.rearrange("b n k -> (b n) k"))
+        bias = keep.tile([P, SAMPLES * LAYERS, PACK], BF16)
+        nc.scalar.dma_start(out=bias[:], in_=params[:, D * D :].rearrange("q (m j) -> m q j", j=PACK))
+        raw = {}
+        for l in range(LAYERS):
+            for b in range(SAMPLES):
+                raw[l, b] = keep.tile([P, PACK, D], BF16, name="raw%d%d" % (l, b))
+                nc.sync.dma_start(
+                    out=raw[l, b][:],
+                    in_=params[LAYERS * b + l, : D * D].rearrange("(p t e) -> p t e", t=PACK, e=D),
+                )
+
+        ident = keep.tile([P, P], F32)
+        make_identity(nc, ident[:])
+        x_words = x_rows[:].bitcast(F32).rearrange("r (p u) -> r u p", u=2)
+        x_t = psum.tile([P, 2, ALL_ROWS], F32)
+        for u in range(2):
+            nc.tensor.transpose(x_t[:, u, :], x_words[:, u, :], ident[:])
+        x_grouped = keep.tile([P, ALL_ROWS * PACK], BF16, align_bytes=64)
+        nc.vector.tensor_copy(
+            out=x_grouped[:].bitcast(F32).rearrange("p (r u) -> p r u", u=2),
+            in_=x_t[:].rearrange("p u r -> p r u"),
+        )
+        x_codes = keep.tile([P, ALL_ROWS], U32, align_bytes=64)
+        x_scales = keep.tile([P, ALL_ROWS], U8, align_bytes=64)
+        nc.vector.quantize_mx(out=x_codes[:].bitcast(FP8X4), scales=x_scales[:], in_=x_grouped[:])
+
+        h_grouped = keep.tile([P, ALL_ROWS, PACK], BF16, align_bytes=64)
+        h_codes = keep.tile([P, ALL_ROWS], U32, align_bytes=64)
+        h_scales = keep.tile([P, ALL_ROWS], U8, align_bytes=64)
+        out_t = keep.tile([P, PACK, ALL_ROWS], F32)
+
+        for l in range(LAYERS):
+            for b in range(SAMPLES):
+                grouped = keep.tile([P, PACK, P, PACK], BF16, name="grouped%d%d" % (l, b), align_bytes=64)
+                codes = keep.tile([P, PACK, P], U32, name="codes%d%d" % (l, b), align_bytes=64)
+                scales = keep.tile([P, PACK, P], U8, name="scales%d%d" % (l, b), align_bytes=64)
+                quantise_weights(nc, raw[l, b], grouped, codes, scales)
+
+                acc = psum.tile([P, PACK, ALL_ROWS], F32, name="acc%d%d" % (l, b))
+                if l == 0:
+                    multiply(nc, acc, codes, scales, x_codes, x_scales)
+                else:
+                    multiply(nc, acc, codes, scales, h_codes, h_scales)
+
+                own = slice(b * ROWS, (b + 1) * ROWS)
+                bias_b = bias[:, LAYERS * b + l, :].unsqueeze(2).to_broadcast([P, PACK, ROWS])
+                if l == 0:
+                    h_sum = keep.tile([P, PACK, ROWS], F32, name="h_sum%d" % b)
+                    nc.vector.tensor_tensor(out=h_sum[:], in0=acc[:, :, own], in1=bias_b, op=ADD)
+                    nc.scalar.activation(
+                        out=h_grouped[:, own, :], in_=h_sum[:].rearrange("p j n -> p n j"), func=RELU
+                    )
+                else:
+                    nc.vector.tensor_tensor(out=out_t[:, :, own], in0=acc[:, :, own], in1=bias_b, op=ADD)
+            if l == 0:
+                nc.vector.quantize_mx(
+                    out=h_codes[:].bitcast(FP8X4),
+                    scales=h_scales[:],
+                    in_=h_grouped[:].rearrange("p n j -> p (n j)"),
+                )
+
+        final = psum.tile([ALL_ROWS, PACK, P], F32)
+        for j in range(PACK):
+            nc.tensor.transpose(final[:, j, :], out_t[:, j, :], ident[:])
+        result = keep.tile([ALL_ROWS, D], F32)
+        nc.scalar.activation(
+            out=result[:].rearrange("r (m j) -> r m j", j=PACK),
+            in_=final[:].rearrange("r j m -> r m j"),
+            func=RELU,
+        )
+        nc.sync.dma_start(out=out.rearrange("b n e -> (b n) e"), in_=result[:])

@@ -23,11 +23,14 @@ VECTOR_BLOCKS = 2
 FLOPS = 2 * SAMPLES * LAYERS * ROWS * D * D
 
 
-def quantise_weights(nc, raw, grouped, codes, scales):
+def regroup_weights(nc, raw, grouped):
     source = raw[:].rearrange("p t (m j) -> p m t j", j=PACK)
     target = grouped[:].rearrange("p j m t -> p m t j")
     nc.vector.tensor_copy(out=target[:, :, :, :VECTOR_BLOCKS], in_=source[:, :, :, :VECTOR_BLOCKS])
     nc.scalar.copy(out=target[:, :, :, VECTOR_BLOCKS:], in_=source[:, :, :, VECTOR_BLOCKS:])
+
+
+def quantise_weights(nc, grouped, codes, scales):
     for blocks in (slice(0, VECTOR_BLOCKS), slice(VECTOR_BLOCKS, PACK)):
         nc.vector.quantize_mx(
             out=codes[:, blocks, :].rearrange("p j m -> p (j m)").bitcast(FP8X4),
@@ -36,7 +39,7 @@ def quantise_weights(nc, raw, grouped, codes, scales):
         )
 
 
-def multiply(nc, acc, codes, scales, act_codes, act_scales):
+def multiply_mx(nc, acc, codes, scales, act_codes, act_scales):
     for j in range(PACK):
         nc.tensor.matmul_mx(
             out=acc[:, j, :],
@@ -56,6 +59,7 @@ def tile_can_s_kernel(tc, user_emb, item_emb, out):
     with ExitStack() as ctx:
         keep = ctx.enter_context(tc.tile_pool(name="keep", bufs=1))
         psum = ctx.enter_context(tc.psum_pool(name="psum", bufs=1))
+        ctx.enter_context(tc.manual_schedule())
 
         x_rows = keep.tile([ALL_ROWS, D], BF16)
         nc.sync.dma_start(out=x_rows[:], in_=user_emb.rearrange("b n k -> (b n) k"))
@@ -89,36 +93,62 @@ def tile_can_s_kernel(tc, user_emb, item_emb, out):
         h_codes = keep.tile([P, ALL_ROWS], U32, align_bytes=64)
         h_scales = keep.tile([P, ALL_ROWS], U8, align_bytes=64)
         out_t = keep.tile([P, PACK, ALL_ROWS], F32)
-
+        grouped, codes, scales, acc, h_sum = {}, {}, {}, {}, {}
         for l in range(LAYERS):
             for b in range(SAMPLES):
-                grouped = keep.tile([P, PACK, P, PACK], BF16, name="grouped%d%d" % (l, b), align_bytes=64)
-                codes = keep.tile([P, PACK, P], U32, name="codes%d%d" % (l, b), align_bytes=64)
-                scales = keep.tile([P, PACK, P], U8, name="scales%d%d" % (l, b), align_bytes=64)
-                quantise_weights(nc, raw[l, b], grouped, codes, scales)
+                tail = "%d%d" % (l, b)
+                grouped[l, b] = keep.tile([P, PACK, P, PACK], BF16, name="grouped" + tail, align_bytes=64)
+                codes[l, b] = keep.tile([P, PACK, P], U32, name="codes" + tail, align_bytes=64)
+                scales[l, b] = keep.tile([P, PACK, P], U8, name="scales" + tail, align_bytes=64)
+                acc[l, b] = psum.tile([P, PACK, ALL_ROWS], F32, name="acc" + tail)
+        for b in range(SAMPLES):
+            h_sum[b] = keep.tile([P, PACK, ROWS], F32, name="h_sum%d" % b)
 
-                acc = psum.tile([P, PACK, ALL_ROWS], F32, name="acc%d%d" % (l, b))
-                if l == 0:
-                    multiply(nc, acc, codes, scales, x_codes, x_scales)
-                else:
-                    multiply(nc, acc, codes, scales, h_codes, h_scales)
+        def regroup(l, b):
+            regroup_weights(nc, raw[l, b], grouped[l, b])
 
-                own = slice(b * ROWS, (b + 1) * ROWS)
-                bias_b = bias[:, LAYERS * b + l, :].unsqueeze(2).to_broadcast([P, PACK, ROWS])
-                if l == 0:
-                    h_sum = keep.tile([P, PACK, ROWS], F32, name="h_sum%d" % b)
-                    nc.vector.tensor_tensor(out=h_sum[:], in0=acc[:, :, own], in1=bias_b, op=ADD)
-                    nc.scalar.activation(
-                        out=h_grouped[:, own, :], in_=h_sum[:].rearrange("p j n -> p n j"), func=RELU
-                    )
-                else:
-                    nc.vector.tensor_tensor(out=out_t[:, :, own], in0=acc[:, :, own], in1=bias_b, op=ADD)
+        def quantise(l, b):
+            quantise_weights(nc, grouped[l, b], codes[l, b], scales[l, b])
+
+        def multiply(l, b):
             if l == 0:
-                nc.vector.quantize_mx(
-                    out=h_codes[:].bitcast(FP8X4),
-                    scales=h_scales[:],
-                    in_=h_grouped[:].rearrange("p n j -> p (n j)"),
-                )
+                multiply_mx(nc, acc[l, b], codes[l, b], scales[l, b], x_codes, x_scales)
+            else:
+                multiply_mx(nc, acc[l, b], codes[l, b], scales[l, b], h_codes, h_scales)
+
+        def add_bias(l, b):
+            own = slice(b * ROWS, (b + 1) * ROWS)
+            bias_b = bias[:, LAYERS * b + l, :].unsqueeze(2).to_broadcast([P, PACK, ROWS])
+            target = h_sum[b][:] if l == 0 else out_t[:, :, own]
+            nc.vector.tensor_tensor(out=target, in0=acc[l, b][:, :, own], in1=bias_b, op=ADD)
+
+        def relu_h(b):
+            own = slice(b * ROWS, (b + 1) * ROWS)
+            nc.scalar.activation(out=h_grouped[:, own, :], in_=h_sum[b][:].rearrange("p j n -> p n j"), func=RELU)
+
+        regroup(0, 0)
+        quantise(0, 0)
+        multiply(0, 0)
+        regroup(0, 1)
+        add_bias(0, 0)
+        quantise(0, 1)
+        multiply(0, 1)
+        relu_h(0)
+        regroup(1, 0)
+        add_bias(0, 1)
+        quantise(1, 0)
+        relu_h(1)
+        regroup(1, 1)
+        nc.vector.quantize_mx(
+            out=h_codes[:].bitcast(FP8X4),
+            scales=h_scales[:],
+            in_=h_grouped[:].rearrange("p n j -> p (n j)"),
+        )
+        multiply(1, 0)
+        quantise(1, 1)
+        multiply(1, 1)
+        add_bias(1, 0)
+        add_bias(1, 1)
 
         final = psum.tile([ALL_ROWS, PACK, P], F32)
         for j in range(PACK):

@@ -14,47 +14,43 @@ RELU = mybir.ActivationFunctionType.Relu
 P = 128
 PACK = 4
 D = P * PACK
+HALF = D // 2
 SAMPLES = 2
 ROWS = 64
 ALL_ROWS = SAMPLES * ROWS
 LAYERS = 2
-VECTOR_BLOCKS = 2
 
 FLOPS = 2 * SAMPLES * LAYERS * ROWS * D * D
 
 
-def regroup_weights(nc, raw, grouped):
+def regroup_layer0(nc, raw, grouped):
     source = raw[:].rearrange("p t (m j) -> p m t j", j=PACK)
-    target = grouped[:].rearrange("p j m t -> p m t j")
-    nc.vector.tensor_copy(out=target[:, :, :, :VECTOR_BLOCKS], in_=source[:, :, :, :VECTOR_BLOCKS])
-    nc.scalar.copy(out=target[:, :, :, VECTOR_BLOCKS:], in_=source[:, :, :, VECTOR_BLOCKS:])
+    target = grouped[:].rearrange("p (j m) t -> p m t j", j=PACK)
+    nc.vector.tensor_copy(out=target[:, :, :, : PACK // 2], in_=source[:, :, :, : PACK // 2])
+    nc.scalar.copy(out=target[:, :, :, PACK // 2 :], in_=source[:, :, :, PACK // 2 :])
+
+
+def regroup_layer1(nc, raw, grouped):
+    source = raw[:].rearrange("p t (c i) -> p c t i", i=PACK)
+    target = grouped[:].rearrange("p (c i) t -> p c t i", i=PACK)
+    middle = HALF // PACK
+    nc.vector.tensor_copy(out=target[:, :middle], in_=source[:, :middle])
+    nc.scalar.copy(out=target[:, middle:], in_=source[:, middle:])
 
 
 def quantise_weights(nc, grouped, codes, scales):
-    for blocks in (slice(0, VECTOR_BLOCKS), slice(VECTOR_BLOCKS, PACK)):
+    for cols in (slice(0, HALF), slice(HALF, D)):
         nc.vector.quantize_mx(
-            out=codes[:, blocks, :].rearrange("p j m -> p (j m)").bitcast(FP8X4),
-            scales=scales[:, blocks, :].rearrange("p j m -> p (j m)"),
-            in_=grouped[:, blocks, :, :].rearrange("p j m t -> p (j m t)"),
-        )
-
-
-def multiply_mx(nc, acc, codes, scales, act_codes, act_scales):
-    for j in range(PACK):
-        nc.tensor.matmul_mx(
-            out=acc[:, j, :],
-            lhsT=codes[:, j, :].bitcast(FP8X4),
-            lhsT_scale=scales[:, j, :],
-            rhs=act_codes[:].bitcast(FP8X4),
-            rhs_scale=act_scales[:],
-            start=True,
-            stop=True,
+            out=codes[:, cols].bitcast(FP8X4),
+            scales=scales[:, cols],
+            in_=grouped[:, cols, :].rearrange("p c t -> p (c t)"),
         )
 
 
 def tile_can_s_kernel(tc, user_emb, item_emb, out):
     nc = tc.nc
     params = item_emb.rearrange("b (l r) -> (b l) r", l=LAYERS)
+    out_rows = out.rearrange("b n e -> (b n) e")
 
     with ExitStack() as ctx:
         keep = ctx.enter_context(tc.tile_pool(name="keep", bufs=1))
@@ -63,19 +59,36 @@ def tile_can_s_kernel(tc, user_emb, item_emb, out):
 
         x_rows = keep.tile([ALL_ROWS, D], BF16)
         nc.sync.dma_start(out=x_rows[:], in_=user_emb.rearrange("b n k -> (b n) k"))
-        bias = keep.tile([P, SAMPLES * LAYERS, PACK], BF16)
-        nc.scalar.dma_start(out=bias[:], in_=params[:, D * D :].rearrange("q (m j) -> m q j", j=PACK))
-        raw = {}
+        bias = keep.tile([P, SAMPLES, LAYERS, PACK], BF16)
+        nc.scalar.dma_start(
+            out=bias[:].rearrange("m b l j -> m (b l) j"),
+            in_=params[:, D * D :].rearrange("q (m j) -> m q j", j=PACK),
+        )
+        raw, grouped, codes, scales = {}, {}, {}, {}
         for l in range(LAYERS):
             for b in range(SAMPLES):
-                raw[l, b] = keep.tile([P, PACK, D], BF16, name="raw%d%d" % (l, b))
+                tail = "%d%d" % (l, b)
+                raw[l, b] = keep.tile([P, PACK, D], BF16, name="raw" + tail)
                 nc.sync.dma_start(
                     out=raw[l, b][:],
                     in_=params[LAYERS * b + l, : D * D].rearrange("(p t e) -> p t e", t=PACK, e=D),
                 )
+                grouped[l, b] = keep.tile([P, D, PACK], BF16, name="grouped" + tail, align_bytes=64)
+                codes[l, b] = keep.tile([P, D], U32, name="codes" + tail, align_bytes=64)
+                scales[l, b] = keep.tile([P, D], U8, name="scales" + tail, align_bytes=64)
 
         ident = keep.tile([P, P], F32)
         make_identity(nc, ident[:])
+
+        h_grouped = keep.tile([P, SAMPLES, ALL_ROWS, PACK], BF16, align_bytes=64)
+        nc.vector.memset(h_grouped[:], 0.0)
+
+        bias_cols = keep.tile([P, PACK, ALL_ROWS], F32)
+        nc.vector.tensor_copy(
+            out=bias_cols[:].rearrange("m j (b n) -> m j b n", b=SAMPLES),
+            in_=bias[:, :, 1, :].rearrange("m b j -> m j b").unsqueeze(3).to_broadcast([P, PACK, SAMPLES, ROWS]),
+        )
+
         x_words = x_rows[:].bitcast(F32).rearrange("r (p u) -> r u p", u=2)
         x_t = psum.tile([P, 2, ALL_ROWS], F32)
         for u in range(2):
@@ -89,74 +102,91 @@ def tile_can_s_kernel(tc, user_emb, item_emb, out):
         x_scales = keep.tile([P, ALL_ROWS], U8, align_bytes=64)
         nc.vector.quantize_mx(out=x_codes[:].bitcast(FP8X4), scales=x_scales[:], in_=x_grouped[:])
 
-        h_grouped = keep.tile([P, ALL_ROWS, PACK], BF16, align_bytes=64)
-        h_codes = keep.tile([P, ALL_ROWS], U32, align_bytes=64)
-        h_scales = keep.tile([P, ALL_ROWS], U8, align_bytes=64)
-        out_t = keep.tile([P, PACK, ALL_ROWS], F32)
-        grouped, codes, scales, acc, h_sum = {}, {}, {}, {}, {}
-        for l in range(LAYERS):
-            for b in range(SAMPLES):
-                tail = "%d%d" % (l, b)
-                grouped[l, b] = keep.tile([P, PACK, P, PACK], BF16, name="grouped" + tail, align_bytes=64)
-                codes[l, b] = keep.tile([P, PACK, P], U32, name="codes" + tail, align_bytes=64)
-                scales[l, b] = keep.tile([P, PACK, P], U8, name="scales" + tail, align_bytes=64)
-                acc[l, b] = psum.tile([P, PACK, ALL_ROWS], F32, name="acc" + tail)
+        bias_t = psum.tile([ALL_ROWS, PACK, P], F32)
+        for j in range(PACK):
+            nc.tensor.transpose(bias_t[:, j, :], bias_cols[:, j, :], ident[:])
+
+        h_t, h_sum = {}, {}
         for b in range(SAMPLES):
+            h_t[b] = psum.tile([P, PACK, ALL_ROWS], F32, name="h_t%d" % b)
             h_sum[b] = keep.tile([P, PACK, ROWS], F32, name="h_sum%d" % b)
 
-        def regroup(l, b):
-            regroup_weights(nc, raw[l, b], grouped[l, b])
+        def multiply_layer0(b):
+            for j in range(PACK):
+                block = slice(j * P, (j + 1) * P)
+                nc.tensor.matmul_mx(
+                    out=h_t[b][:, j, :],
+                    lhsT=codes[0, b][:, block].bitcast(FP8X4),
+                    lhsT_scale=scales[0, b][:, block],
+                    rhs=x_codes[:].bitcast(FP8X4),
+                    rhs_scale=x_scales[:],
+                    start=True,
+                    stop=True,
+                )
 
-        def quantise(l, b):
-            quantise_weights(nc, grouped[l, b], codes[l, b], scales[l, b])
-
-        def multiply(l, b):
-            if l == 0:
-                multiply_mx(nc, acc[l, b], codes[l, b], scales[l, b], x_codes, x_scales)
-            else:
-                multiply_mx(nc, acc[l, b], codes[l, b], scales[l, b], h_codes, h_scales)
-
-        def add_bias(l, b):
+        def add_bias_layer0(b):
             own = slice(b * ROWS, (b + 1) * ROWS)
-            bias_b = bias[:, LAYERS * b + l, :].unsqueeze(2).to_broadcast([P, PACK, ROWS])
-            target = h_sum[b][:] if l == 0 else out_t[:, :, own]
-            nc.vector.tensor_tensor(out=target, in0=acc[l, b][:, :, own], in1=bias_b, op=ADD)
+            nc.vector.tensor_tensor(
+                out=h_sum[b][:],
+                in0=h_t[b][:, :, own],
+                in1=bias[:, b, 0, :].unsqueeze(2).to_broadcast([P, PACK, ROWS]),
+                op=ADD,
+            )
 
-        def relu_h(b):
+        def relu_layer0(b):
             own = slice(b * ROWS, (b + 1) * ROWS)
-            nc.scalar.activation(out=h_grouped[:, own, :], in_=h_sum[b][:].rearrange("p j n -> p n j"), func=RELU)
+            nc.scalar.activation(
+                out=h_grouped[:, b, own, :], in_=h_sum[b][:].rearrange("p j n -> p n j"), func=RELU
+            )
 
-        regroup(0, 0)
-        quantise(0, 0)
-        multiply(0, 0)
-        regroup(0, 1)
-        add_bias(0, 0)
-        quantise(0, 1)
-        multiply(0, 1)
-        relu_h(0)
-        regroup(1, 0)
-        add_bias(0, 1)
-        quantise(1, 0)
-        relu_h(1)
-        regroup(1, 1)
+        h_codes = keep.tile([P, SAMPLES, ALL_ROWS], U32, align_bytes=64)
+        h_scales = keep.tile([P, SAMPLES, ALL_ROWS], U8, align_bytes=64)
+        product = psum.tile([ALL_ROWS, D], F32)
+
+        def multiply_layer1(b):
+            nc.tensor.matmul_mx(
+                out=product[:],
+                lhsT=h_codes[:, b, :].bitcast(FP8X4),
+                lhsT_scale=h_scales[:, b, :],
+                rhs=codes[1, b][:].bitcast(FP8X4),
+                rhs_scale=scales[1, b][:],
+                start=(b == 0),
+                stop=(b == SAMPLES - 1),
+            )
+
+        regroup_layer0(nc, raw[0, 0], grouped[0, 0])
+        quantise_weights(nc, grouped[0, 0], codes[0, 0], scales[0, 0])
+        multiply_layer0(0)
+        regroup_layer0(nc, raw[0, 1], grouped[0, 1])
+        add_bias_layer0(0)
+        quantise_weights(nc, grouped[0, 1], codes[0, 1], scales[0, 1])
+        multiply_layer0(1)
+        relu_layer0(0)
+        regroup_layer1(nc, raw[1, 0], grouped[1, 0])
+        add_bias_layer0(1)
+        quantise_weights(nc, grouped[1, 0], codes[1, 0], scales[1, 0])
+        relu_layer0(1)
+        regroup_layer1(nc, raw[1, 1], grouped[1, 1])
         nc.vector.quantize_mx(
-            out=h_codes[:].bitcast(FP8X4),
-            scales=h_scales[:],
-            in_=h_grouped[:].rearrange("p n j -> p (n j)"),
+            out=h_codes[:].rearrange("p b r -> p (b r)").bitcast(FP8X4),
+            scales=h_scales[:].rearrange("p b r -> p (b r)"),
+            in_=h_grouped[:].rearrange("p b r j -> p (b r j)"),
         )
-        multiply(1, 0)
-        quantise(1, 1)
-        multiply(1, 1)
-        add_bias(1, 0)
-        add_bias(1, 1)
+        multiply_layer1(0)
+        quantise_weights(nc, grouped[1, 1], codes[1, 1], scales[1, 1])
+        multiply_layer1(1)
 
-        final = psum.tile([ALL_ROWS, PACK, P], F32)
-        for j in range(PACK):
-            nc.tensor.transpose(final[:, j, :], out_t[:, j, :], ident[:])
-        result = keep.tile([ALL_ROWS, D], F32)
-        nc.scalar.activation(
-            out=result[:].rearrange("r (m j) -> r m j", j=PACK),
-            in_=final[:].rearrange("r j m -> r m j"),
-            func=RELU,
+        bias_rows = keep.tile([ALL_ROWS, D], F32)
+        nc.scalar.copy(
+            out=bias_rows[:].rearrange("r (m j) -> r m j", j=PACK), in_=bias_t[:].rearrange("r j m -> r m j")
         )
-        nc.sync.dma_start(out=out.rearrange("b n e -> (b n) e"), in_=result[:])
+
+        first, second = slice(0, HALF), slice(HALF, D)
+        summed = keep.tile([ALL_ROWS, D], F32)
+        result = keep.tile([ALL_ROWS, D], F32)
+        nc.vector.tensor_tensor(out=summed[:, first], in0=product[:, first], in1=bias_rows[:, first], op=ADD)
+        nc.scalar.activation(out=result[:, first], in_=summed[:, first], func=RELU)
+        nc.sync.dma_start(out=out_rows[:, first], in_=result[:, first])
+        nc.vector.tensor_tensor(out=summed[:, second], in0=product[:, second], in1=bias_rows[:, second], op=ADD)
+        nc.vector.tensor_scalar_max(out=result[:, second], in0=summed[:, second], scalar1=0.0)
+        nc.sync.dma_start(out=out_rows[:, second], in_=result[:, second])

@@ -38,13 +38,12 @@ def regroup_layer1(nc, raw, grouped):
     nc.scalar.copy(out=target[:, middle:], in_=source[:, middle:])
 
 
-def quantise_weights(nc, grouped, codes, scales):
-    for cols in (slice(0, HALF), slice(HALF, D)):
-        nc.vector.quantize_mx(
-            out=codes[:, cols].bitcast(FP8X4),
-            scales=scales[:, cols],
-            in_=grouped[:, cols, :].rearrange("p c t -> p (c t)"),
-        )
+def quantise_half(nc, grouped, codes, scales, cols):
+    nc.vector.quantize_mx(
+        out=codes[:, cols].bitcast(FP8X4),
+        scales=scales[:, cols],
+        in_=grouped[:, cols, :].rearrange("p c t -> p (c t)"),
+    )
 
 
 def tile_can_s_kernel(tc, user_emb, item_emb, out):
@@ -154,26 +153,42 @@ def tile_can_s_kernel(tc, user_emb, item_emb, out):
                 stop=(b == SAMPLES - 1),
             )
 
-        regroup_layer0(nc, raw[0, 0], grouped[0, 0])
-        quantise_weights(nc, grouped[0, 0], codes[0, 0], scales[0, 0])
+        def regroup(l, b):
+            if l == 0:
+                regroup_layer0(nc, raw[l, b], grouped[l, b])
+            else:
+                regroup_layer1(nc, raw[l, b], grouped[l, b])
+
+        def quantise_vectors_half(l, b):
+            quantise_half(nc, grouped[l, b], codes[l, b], scales[l, b], slice(0, HALF))
+
+        def quantise_scalars_half(l, b):
+            quantise_half(nc, grouped[l, b], codes[l, b], scales[l, b], slice(HALF, D))
+
+        regroup(0, 0)
+        quantise_vectors_half(0, 0)
+        regroup(0, 1)
+        quantise_scalars_half(0, 0)
         multiply_layer0(0)
-        regroup_layer0(nc, raw[0, 1], grouped[0, 1])
-        add_bias_layer0(0)
-        quantise_weights(nc, grouped[0, 1], codes[0, 1], scales[0, 1])
+        quantise_vectors_half(0, 1)
+        quantise_scalars_half(0, 1)
         multiply_layer0(1)
+        regroup(1, 0)
+        add_bias_layer0(0)
         relu_layer0(0)
-        regroup_layer1(nc, raw[1, 0], grouped[1, 0])
         add_bias_layer0(1)
-        quantise_weights(nc, grouped[1, 0], codes[1, 0], scales[1, 0])
         relu_layer0(1)
-        regroup_layer1(nc, raw[1, 1], grouped[1, 1])
+        quantise_vectors_half(1, 0)
+        regroup(1, 1)
+        quantise_scalars_half(1, 0)
         nc.vector.quantize_mx(
             out=h_codes[:].rearrange("p b r -> p (b r)").bitcast(FP8X4),
             scales=h_scales[:].rearrange("p b r -> p (b r)"),
             in_=h_grouped[:].rearrange("p b r j -> p (b r j)"),
         )
         multiply_layer1(0)
-        quantise_weights(nc, grouped[1, 1], codes[1, 1], scales[1, 1])
+        quantise_vectors_half(1, 1)
+        quantise_scalars_half(1, 1)
         multiply_layer1(1)
 
         bias_rows = keep.tile([ALL_ROWS, D], F32)

@@ -15,6 +15,8 @@ P = 128
 PACK = 4
 D = P * PACK
 HALF = D // 2
+HALVES = (slice(0, HALF), slice(HALF, D))
+BANK = 512
 SAMPLES = 2
 ROWS = 64
 ALL_ROWS = SAMPLES * ROWS
@@ -140,15 +142,16 @@ def tile_can_s_kernel(tc, user_emb, item_emb, out):
 
         h_codes = keep.tile([P, SAMPLES, ALL_ROWS], U32, align_bytes=64)
         h_scales = keep.tile([P, SAMPLES, ALL_ROWS], U8, align_bytes=64)
-        product = psum.tile([ALL_ROWS, D], F32)
+        product = [psum.tile([ALL_ROWS, BANK], F32, name="product%d" % c) for c in range(len(HALVES))]
 
-        def multiply_layer1(b):
+        def multiply_layer1(b, c):
+            cols = HALVES[c]
             nc.tensor.matmul_mx(
-                out=product[:],
+                out=product[c][:, :HALF],
                 lhsT=h_codes[:, b, :].bitcast(FP8X4),
                 lhsT_scale=h_scales[:, b, :],
-                rhs=codes[1, b][:].bitcast(FP8X4),
-                rhs_scale=scales[1, b][:],
+                rhs=codes[1, b][:, cols].bitcast(FP8X4),
+                rhs_scale=scales[1, b][:, cols],
                 start=(b == 0),
                 stop=(b == SAMPLES - 1),
             )
@@ -160,10 +163,10 @@ def tile_can_s_kernel(tc, user_emb, item_emb, out):
                 regroup_layer1(nc, raw[l, b], grouped[l, b])
 
         def quantise_vectors_half(l, b):
-            quantise_half(nc, grouped[l, b], codes[l, b], scales[l, b], slice(0, HALF))
+            quantise_half(nc, grouped[l, b], codes[l, b], scales[l, b], HALVES[0])
 
         def quantise_scalars_half(l, b):
-            quantise_half(nc, grouped[l, b], codes[l, b], scales[l, b], slice(HALF, D))
+            quantise_half(nc, grouped[l, b], codes[l, b], scales[l, b], HALVES[1])
 
         regroup(0, 0)
         quantise_vectors_half(0, 0)
@@ -186,22 +189,24 @@ def tile_can_s_kernel(tc, user_emb, item_emb, out):
             scales=h_scales[:].rearrange("p b r -> p (b r)"),
             in_=h_grouped[:].rearrange("p b r j -> p (b r j)"),
         )
-        multiply_layer1(0)
+        multiply_layer1(0, 0)
+        multiply_layer1(0, 1)
         quantise_vectors_half(1, 1)
+        multiply_layer1(1, 0)
         quantise_scalars_half(1, 1)
-        multiply_layer1(1)
+        multiply_layer1(1, 1)
 
         bias_rows = keep.tile([ALL_ROWS, D], F32)
         nc.scalar.copy(
             out=bias_rows[:].rearrange("r (m j) -> r m j", j=PACK), in_=bias_t[:].rearrange("r j m -> r m j")
         )
 
-        first, second = slice(0, HALF), slice(HALF, D)
+        first, second = HALVES
         summed = keep.tile([ALL_ROWS, D], F32)
         result = keep.tile([ALL_ROWS, D], F32)
-        nc.vector.tensor_tensor(out=summed[:, first], in0=product[:, first], in1=bias_rows[:, first], op=ADD)
+        nc.vector.tensor_tensor(out=summed[:, first], in0=product[0][:, :HALF], in1=bias_rows[:, first], op=ADD)
         nc.scalar.activation(out=result[:, first], in_=summed[:, first], func=RELU)
         nc.sync.dma_start(out=out_rows[:, first], in_=result[:, first])
-        nc.vector.tensor_tensor(out=summed[:, second], in0=product[:, second], in1=bias_rows[:, second], op=ADD)
+        nc.vector.tensor_tensor(out=summed[:, second], in0=product[1][:, :HALF], in1=bias_rows[:, second], op=ADD)
         nc.vector.tensor_scalar_max(out=result[:, second], in0=summed[:, second], scalar1=0.0)
         nc.sync.dma_start(out=out_rows[:, second], in_=result[:, second])

@@ -85,7 +85,7 @@ def tile_can_s_kernel(tc, user_emb, item_emb, out):
         nc.vector.memset(h_grouped[:], 0.0)
 
         bias_cols = keep.tile([P, PACK, ALL_ROWS], F32)
-        nc.vector.tensor_copy(
+        nc.scalar.copy(
             out=bias_cols[:].rearrange("m j (b n) -> m j b n", b=SAMPLES),
             in_=bias[:, :, 1, :].rearrange("m b j -> m j b").unsqueeze(3).to_broadcast([P, PACK, SAMPLES, ROWS]),
         )
@@ -197,9 +197,12 @@ def tile_can_s_kernel(tc, user_emb, item_emb, out):
         multiply_layer1(1, 1)
 
         bias_rows = keep.tile([ALL_ROWS, D], F32)
-        nc.scalar.copy(
-            out=bias_rows[:].rearrange("r (m j) -> r m j", j=PACK), in_=bias_t[:].rearrange("r j m -> r m j")
-        )
+        for c in range(len(HALVES)):
+            features = slice(c * P // 2, (c + 1) * P // 2)
+            nc.scalar.copy(
+                out=bias_rows[:, HALVES[c]].rearrange("r (m j) -> r m j", j=PACK),
+                in_=bias_t[:, :, features].rearrange("r j m -> r m j"),
+            )
 
         first, second = HALVES
         summed = keep.tile([ALL_ROWS, D], F32)

@@ -58,13 +58,13 @@ def tile_can_s_kernel(tc, user_emb, item_emb, out):
         psum = ctx.enter_context(tc.psum_pool(name="psum", bufs=1))
         ctx.enter_context(tc.manual_schedule())
 
-        x_rows = keep.tile([ALL_ROWS, D], BF16)
-        nc.sync.dma_start(out=x_rows[:], in_=user_emb.rearrange("b n k -> (b n) k"))
         bias = keep.tile([P, SAMPLES, LAYERS, PACK], BF16)
-        nc.scalar.dma_start(
+        nc.sync.dma_start(
             out=bias[:].rearrange("m b l j -> m (b l) j"),
             in_=params[:, D * D :].rearrange("q (m j) -> m q j", j=PACK),
         )
+        x_rows = keep.tile([ALL_ROWS, D], BF16)
+        nc.sync.dma_start(out=x_rows[:], in_=user_emb.rearrange("b n k -> (b n) k"))
         raw, grouped, codes, scales = {}, {}, {}, {}
         for l in range(LAYERS):
             for b in range(SAMPLES):
@@ -85,7 +85,7 @@ def tile_can_s_kernel(tc, user_emb, item_emb, out):
         nc.vector.memset(h_grouped[:], 0.0)
 
         bias_cols = keep.tile([P, PACK, ALL_ROWS], F32)
-        nc.scalar.copy(
+        nc.vector.tensor_copy(
             out=bias_cols[:].rearrange("m j (b n) -> m j b n", b=SAMPLES),
             in_=bias[:, :, 1, :].rearrange("m b j -> m j b").unsqueeze(3).to_broadcast([P, PACK, SAMPLES, ROWS]),
         )
@@ -197,12 +197,9 @@ def tile_can_s_kernel(tc, user_emb, item_emb, out):
         multiply_layer1(1, 1)
 
         bias_rows = keep.tile([ALL_ROWS, D], F32)
-        for c in range(len(HALVES)):
-            features = slice(c * P // 2, (c + 1) * P // 2)
-            nc.scalar.copy(
-                out=bias_rows[:, HALVES[c]].rearrange("r (m j) -> r m j", j=PACK),
-                in_=bias_t[:, :, features].rearrange("r j m -> r m j"),
-            )
+        nc.scalar.copy(
+            out=bias_rows[:].rearrange("r (m j) -> r m j", j=PACK), in_=bias_t[:].rearrange("r j m -> r m j")
+        )
 
         first, second = HALVES
         summed = keep.tile([ALL_ROWS, D], F32)

@@ -7,6 +7,7 @@ F32 = mybir.dt.float32
 BF16 = mybir.dt.bfloat16
 U32 = mybir.dt.uint32
 U8 = mybir.dt.uint8
+I32 = mybir.dt.int32
 FP8X4 = mybir.dt.float8_e4m3fn_x4
 ADD = mybir.AluOpType.add
 RELU = mybir.ActivationFunctionType.Relu
@@ -81,8 +82,11 @@ def tile_can_s_kernel(tc, user_emb, item_emb, out):
         ident = keep.tile([P, P], F32)
         make_identity(nc, ident[:])
 
-        h_grouped = keep.tile([P, SAMPLES, ALL_ROWS, PACK], BF16, align_bytes=64)
-        nc.vector.memset(h_grouped[:], 0.0)
+        h_codes = keep.tile([P, SAMPLES * ALL_ROWS], U32, align_bytes=64)
+        h_scales = keep.tile([P, SAMPLES * ALL_ROWS], U8, align_bytes=64)
+        nc.vector.memset(h_codes[:].bitcast(I32), 0)
+        nc.vector.memset(h_scales[:].bitcast(I32), 0)
+        h_grouped = keep.tile([P, SAMPLES, ROWS, PACK], BF16, align_bytes=64)
 
         bias_cols = keep.tile([P, PACK, ALL_ROWS], F32)
         nc.vector.tensor_copy(
@@ -135,21 +139,19 @@ def tile_can_s_kernel(tc, user_emb, item_emb, out):
             )
 
         def relu_layer0(b):
-            own = slice(b * ROWS, (b + 1) * ROWS)
             nc.scalar.activation(
-                out=h_grouped[:, b, own, :], in_=h_sum[b][:].rearrange("p j n -> p n j"), func=RELU
+                out=h_grouped[:, SAMPLES - 1 - b, :, :], in_=h_sum[b][:].rearrange("p j n -> p n j"), func=RELU
             )
 
-        h_codes = keep.tile([P, SAMPLES, ALL_ROWS], U32, align_bytes=64)
-        h_scales = keep.tile([P, SAMPLES, ALL_ROWS], U8, align_bytes=64)
         product = [psum.tile([ALL_ROWS, BANK], F32, name="product%d" % c) for c in range(len(HALVES))]
 
         def multiply_layer1(b, c):
             cols = HALVES[c]
+            rows = slice((SAMPLES - 1 - b) * ALL_ROWS, (SAMPLES - b) * ALL_ROWS)
             nc.tensor.matmul_mx(
                 out=product[c][:, :HALF],
-                lhsT=h_codes[:, b, :].bitcast(FP8X4),
-                lhsT_scale=h_scales[:, b, :],
+                lhsT=h_codes[:, rows].bitcast(FP8X4),
+                lhsT_scale=h_scales[:, rows],
                 rhs=codes[1, b][:, cols].bitcast(FP8X4),
                 rhs_scale=scales[1, b][:, cols],
                 start=(b == 0),
@@ -184,10 +186,11 @@ def tile_can_s_kernel(tc, user_emb, item_emb, out):
         quantise_vectors_half(1, 0)
         regroup(1, 1)
         quantise_scalars_half(1, 0)
+        live = slice(ROWS, ROWS + ALL_ROWS)
         nc.vector.quantize_mx(
-            out=h_codes[:].rearrange("p b r -> p (b r)").bitcast(FP8X4),
-            scales=h_scales[:].rearrange("p b r -> p (b r)"),
-            in_=h_grouped[:].rearrange("p b r j -> p (b r j)"),
+            out=h_codes[:, live].bitcast(FP8X4),
+            scales=h_scales[:, live],
+            in_=h_grouped[:].rearrange("p b n j -> p (b n j)"),
         )
         multiply_layer1(0, 0)
         multiply_layer1(0, 1)

@@ -33,12 +33,11 @@ def regroup_layer0(nc, raw, grouped):
     nc.scalar.copy(out=target[:, :, :, PACK // 2 :], in_=source[:, :, :, PACK // 2 :])
 
 
-def regroup_layer1(nc, raw, grouped):
+def regroup_layer1(copy, raw, grouped, cols):
     source = raw[:].rearrange("p t (c i) -> p c t i", i=PACK)
     target = grouped[:].rearrange("p (c i) t -> p c t i", i=PACK)
-    middle = HALF // PACK
-    nc.vector.tensor_copy(out=target[:, :middle], in_=source[:, :middle])
-    nc.scalar.copy(out=target[:, middle:], in_=source[:, middle:])
+    runs = slice(cols.start // PACK, cols.stop // PACK)
+    copy(out=target[:, runs], in_=source[:, runs])
 
 
 def quantise_half(nc, grouped, codes, scales, cols):
@@ -159,10 +158,13 @@ def tile_can_s_kernel(tc, user_emb, item_emb, out):
             )
 
         def regroup(l, b):
-            if l == 0:
-                regroup_layer0(nc, raw[l, b], grouped[l, b])
-            else:
-                regroup_layer1(nc, raw[l, b], grouped[l, b])
+            regroup_layer0(nc, raw[l, b], grouped[l, b])
+
+        def vector_regroups(b, cols):
+            regroup_layer1(nc.vector.tensor_copy, raw[1, b], grouped[1, b], cols)
+
+        def scalar_regroups(b, cols):
+            regroup_layer1(nc.scalar.copy, raw[1, b], grouped[1, b], cols)
 
         def quantise_vectors_half(l, b):
             quantise_half(nc, grouped[l, b], codes[l, b], scales[l, b], HALVES[0])
@@ -178,13 +180,16 @@ def tile_can_s_kernel(tc, user_emb, item_emb, out):
         quantise_vectors_half(0, 1)
         quantise_scalars_half(0, 1)
         multiply_layer0(1)
-        regroup(1, 0)
+        vector_regroups(0, HALVES[0])
+        scalar_regroups(0, HALVES[1])
+        scalar_regroups(1, slice(HALF, HALF + HALF // 2))
         add_bias_layer0(0)
         relu_layer0(0)
         add_bias_layer0(1)
         relu_layer0(1)
         quantise_vectors_half(1, 0)
-        regroup(1, 1)
+        vector_regroups(1, HALVES[0])
+        scalar_regroups(1, slice(HALF + HALF // 2, D))
         quantise_scalars_half(1, 0)
         live = slice(ROWS, ROWS + ALL_ROWS)
         nc.vector.quantize_mx(

@@ -17,6 +17,7 @@ PACK = 4
 D = P * PACK
 HALF = D // 2
 HALVES = (slice(0, HALF), slice(HALF, D))
+VECTORS_COLUMNS = 3 * D // 8
 BANK = 512
 SAMPLES = 2
 ROWS = 64
@@ -180,8 +181,8 @@ def tile_can_s_kernel(tc, user_emb, item_emb, out):
         quantise_vectors_half(0, 1)
         quantise_scalars_half(0, 1)
         multiply_layer0(1)
-        vector_regroups(0, HALVES[0])
-        scalar_regroups(0, HALVES[1])
+        vector_regroups(0, slice(0, VECTORS_COLUMNS))
+        scalar_regroups(0, slice(VECTORS_COLUMNS, D))
         scalar_regroups(1, slice(HALF, HALF + HALF // 2))
         add_bias_layer0(0)
         relu_layer0(0)

@@ -59,13 +59,13 @@ def tile_can_s_kernel(tc, user_emb, item_emb, out):
         psum = ctx.enter_context(tc.psum_pool(name="psum", bufs=1))
         ctx.enter_context(tc.manual_schedule())
 
+        x_rows = keep.tile([ALL_ROWS, D], BF16)
+        nc.sync.dma_start(out=x_rows[:], in_=user_emb.rearrange("b n k -> (b n) k"))
         bias = keep.tile([P, SAMPLES, LAYERS, PACK], BF16)
         nc.sync.dma_start(
             out=bias[:].rearrange("m b l j -> m (b l) j"),
             in_=params[:, D * D :].rearrange("q (m j) -> m q j", j=PACK),
         )
-        x_rows = keep.tile([ALL_ROWS, D], BF16)
-        nc.sync.dma_start(out=x_rows[:], in_=user_emb.rearrange("b n k -> (b n) k"))
         raw, grouped, codes, scales = {}, {}, {}, {}
         for l in range(LAYERS):
             for b in range(SAMPLES):

@@ -158,6 +158,19 @@ def tile_can_s_kernel(tc, user_emb, item_emb, out):
                 stop=(b == SAMPLES - 1),
             )
 
+        idle_bank = psum.tile([ALL_ROWS, BANK], F32)
+
+        def keep_tensor_engine_busy(b):
+            nc.tensor.matmul_mx(
+                out=idle_bank[:],
+                lhsT=x_codes[:].bitcast(FP8X4),
+                lhsT_scale=x_scales[:],
+                rhs=codes[0, b][:].bitcast(FP8X4),
+                rhs_scale=scales[0, b][:],
+                start=True,
+                stop=True,
+            )
+
         def regroup(l, b):
             regroup_layer0(nc, raw[l, b], grouped[l, b])
 
@@ -181,6 +194,8 @@ def tile_can_s_kernel(tc, user_emb, item_emb, out):
         quantise_vectors_half(0, 1)
         quantise_scalars_half(0, 1)
         multiply_layer0(1)
+        for b in (0, 1, 0, 1):
+            keep_tensor_engine_busy(b)
         vector_regroups(0, slice(0, VECTORS_COLUMNS))
         scalar_regroups(0, slice(VECTORS_COLUMNS, D))
         scalar_regroups(1, slice(HALF, HALF + HALF // 2))

@@ -81,6 +81,8 @@ def tile_can_s_kernel(tc, user_emb, item_emb, out):
 
         ident = keep.tile([P, P], F32)
         make_identity(nc, ident[:])
+        ident_bf16 = keep.tile([P, P], BF16)
+        make_identity(nc, ident_bf16[:])
 
         h_codes = keep.tile([P, SAMPLES * ALL_ROWS], U32, align_bytes=64)
         h_scales = keep.tile([P, SAMPLES * ALL_ROWS], U8, align_bytes=64)
@@ -88,7 +90,8 @@ def tile_can_s_kernel(tc, user_emb, item_emb, out):
         nc.vector.memset(h_scales[:].bitcast(I32), 0)
         h_grouped = keep.tile([P, SAMPLES, ROWS, PACK], BF16, align_bytes=64)
 
-        bias_cols = keep.tile([P, PACK, ALL_ROWS], F32)
+        bias_cols = keep.tile([P, PACK, ALL_ROWS], BF16)
+
         nc.vector.tensor_copy(
             out=bias_cols[:].rearrange("m j (b n) -> m j b n", b=SAMPLES),
             in_=bias[:, :, 1, :].rearrange("m b j -> m j b").unsqueeze(3).to_broadcast([P, PACK, SAMPLES, ROWS]),
@@ -107,9 +110,10 @@ def tile_can_s_kernel(tc, user_emb, item_emb, out):
         x_scales = keep.tile([P, ALL_ROWS], U8, align_bytes=64)
         nc.vector.quantize_mx(out=x_codes[:].bitcast(FP8X4), scales=x_scales[:], in_=x_grouped[:])
 
-        bias_t = psum.tile([ALL_ROWS, PACK, P], F32)
+        bias_t = psum.tile([ALL_ROWS, PACK, P], BF16)
         for j in range(PACK):
-            nc.tensor.transpose(bias_t[:, j, :], bias_cols[:, j, :], ident[:])
+            nc.tensor.transpose(bias_t[:, j, :], bias_cols[:, j, :], ident_bf16[:])
+        bias_rows = keep.tile([ALL_ROWS, PACK, P], BF16)
 
         h_t, h_sum = {}, {}
         for b in range(SAMPLES):
@@ -187,6 +191,7 @@ def tile_can_s_kernel(tc, user_emb, item_emb, out):
             quantise_half(nc, grouped[l, b], codes[l, b], scales[l, b], HALVES[1])
 
         regroup(0, 0)
+        nc.vector.tensor_copy(out=bias_rows[:], in_=bias_t[:])
         quantise_vectors_half(0, 0)
         regroup(0, 1)
         quantise_scalars_half(0, 0)
@@ -220,17 +225,22 @@ def tile_can_s_kernel(tc, user_emb, item_emb, out):
         quantise_scalars_half(1, 1)
         multiply_layer1(1, 1)
 
-        bias_rows = keep.tile([ALL_ROWS, D], F32)
-        nc.scalar.copy(
-            out=bias_rows[:].rearrange("r (m j) -> r m j", j=PACK), in_=bias_t[:].rearrange("r j m -> r m j")
-        )
-
         first, second = HALVES
         summed = keep.tile([ALL_ROWS, D], F32)
         result = keep.tile([ALL_ROWS, D], F32)
-        nc.vector.tensor_tensor(out=summed[:, first], in0=product[0][:, :HALF], in1=bias_rows[:, first], op=ADD)
+
+        def add_bias_layer1(c):
+            half = slice(c * P // 2, (c + 1) * P // 2)
+            nc.vector.tensor_tensor(
+                out=summed[:, HALVES[c]].rearrange("r (m j) -> r m j", j=PACK),
+                in0=product[c][:, :HALF].rearrange("r (m j) -> r m j", j=PACK),
+                in1=bias_rows[:, :, half].rearrange("r j m -> r m j"),
+                op=ADD,
+            )
+
+        add_bias_layer1(0)
         nc.scalar.activation(out=result[:, first], in_=summed[:, first], func=RELU)
         nc.sync.dma_start(out=out_rows[:, first], in_=result[:, first])
-        nc.vector.tensor_tensor(out=summed[:, second], in0=product[1][:, :HALF], in1=bias_rows[:, second], op=ADD)
+        add_bias_layer1(1)
         nc.vector.tensor_scalar_max(out=result[:, second], in0=summed[:, second], scalar1=0.0)
         nc.sync.dma_start(out=out_rows[:, second], in_=result[:, second])

@@ -17,7 +17,7 @@ PACK = 4
 D = P * PACK
 HALF = D // 2
 HALVES = (slice(0, HALF), slice(HALF, D))
-VECTORS_COLUMNS = 3 * D // 8
+VECTORS_COLUMNS = D // 4
 BANK = 512
 SAMPLES = 2
 ROWS = 64
@@ -88,6 +88,7 @@ def tile_can_s_kernel(tc, user_emb, item_emb, out):
         h_scales = keep.tile([P, SAMPLES * ALL_ROWS], U8, align_bytes=64)
         nc.vector.memset(h_codes[:].bitcast(I32), 0)
         nc.vector.memset(h_scales[:].bitcast(I32), 0)
+        h_sum = keep.tile([P, SAMPLES, ROWS, PACK], BF16, align_bytes=64)
         h_grouped = keep.tile([P, SAMPLES, ROWS, PACK], BF16, align_bytes=64)
 
         bias_cols = keep.tile([P, PACK, ALL_ROWS], BF16)
@@ -115,10 +116,9 @@ def tile_can_s_kernel(tc, user_emb, item_emb, out):
             nc.tensor.transpose(bias_t[:, j, :], bias_cols[:, j, :], ident_bf16[:])
         bias_rows = keep.tile([ALL_ROWS, PACK, P], BF16)
 
-        h_t, h_sum = {}, {}
+        h_t = {}
         for b in range(SAMPLES):
             h_t[b] = psum.tile([P, PACK, ALL_ROWS], F32, name="h_t%d" % b)
-            h_sum[b] = keep.tile([P, PACK, ROWS], F32, name="h_sum%d" % b)
 
         def multiply_layer0(b):
             for j in range(PACK):
@@ -136,15 +136,17 @@ def tile_can_s_kernel(tc, user_emb, item_emb, out):
         def add_bias_layer0(b):
             own = slice(b * ROWS, (b + 1) * ROWS)
             nc.vector.tensor_tensor(
-                out=h_sum[b][:],
-                in0=h_t[b][:, :, own],
-                in1=bias[:, b, 0, :].unsqueeze(2).to_broadcast([P, PACK, ROWS]),
+                out=h_sum[:, SAMPLES - 1 - b, :, :],
+                in0=h_t[b][:, :, own].rearrange("p j n -> p n j"),
+                in1=bias[:, b, 0, :].unsqueeze(1).to_broadcast([P, ROWS, PACK]),
                 op=ADD,
             )
 
-        def relu_layer0(b):
-            nc.scalar.activation(
-                out=h_grouped[:, SAMPLES - 1 - b, :, :], in_=h_sum[b][:].rearrange("p j n -> p n j"), func=RELU
+        def relu_layer0():
+            nc.vector.tensor_scalar_max(
+                out=h_grouped[:].rearrange("p b n j -> p (b n j)"),
+                in0=h_sum[:].rearrange("p b n j -> p (b n j)"),
+                scalar1=0.0,
             )
 
         product = [psum.tile([ALL_ROWS, BANK], F32, name="product%d" % c) for c in range(len(HALVES))]
@@ -202,15 +204,15 @@ def tile_can_s_kernel(tc, user_emb, item_emb, out):
         for b in (0, 1, 0, 1):
             keep_tensor_engine_busy(b)
         vector_regroups(0, slice(0, VECTORS_COLUMNS))
-        scalar_regroups(0, slice(VECTORS_COLUMNS, D))
-        scalar_regroups(1, slice(HALF, HALF + HALF // 2))
+        scalar_regroups(0, slice(VECTORS_COLUMNS, HALF))
+        scalar_regroups(0, HALVES[1])
         add_bias_layer0(0)
-        relu_layer0(0)
-        add_bias_layer0(1)
-        relu_layer0(1)
         quantise_vectors_half(1, 0)
-        vector_regroups(1, HALVES[0])
-        scalar_regroups(1, slice(HALF + HALF // 2, D))
+        add_bias_layer0(1)
+        vector_regroups(1, slice(0, HALF - D // 8))
+        scalar_regroups(1, slice(HALF - D // 8, HALF))
+        scalar_regroups(1, HALVES[1])
+        relu_layer0()
         quantise_scalars_half(1, 0)
         live = slice(ROWS, ROWS + ALL_ROWS)
         nc.vector.quantize_mx(
@@ -229,18 +231,20 @@ def tile_can_s_kernel(tc, user_emb, item_emb, out):
         summed = keep.tile([ALL_ROWS, D], F32)
         result = keep.tile([ALL_ROWS, D], F32)
 
-        def add_bias_layer1(c):
-            half = slice(c * P // 2, (c + 1) * P // 2)
+        def add_bias_layer1(c, start, width):
+            cols = slice(c * HALF + start, c * HALF + start + width)
             nc.vector.tensor_tensor(
-                out=summed[:, HALVES[c]].rearrange("r (m j) -> r m j", j=PACK),
-                in0=product[c][:, :HALF].rearrange("r (m j) -> r m j", j=PACK),
-                in1=bias_rows[:, :, half].rearrange("r j m -> r m j"),
+                out=summed[:, cols].rearrange("r (m j) -> r m j", j=PACK),
+                in0=product[c][:, start : start + width].rearrange("r (m j) -> r m j", j=PACK),
+                in1=bias_rows[:, :, cols.start // PACK : cols.stop // PACK].rearrange("r j m -> r m j"),
                 op=ADD,
             )
 
-        add_bias_layer1(0)
-        nc.scalar.activation(out=result[:, first], in_=summed[:, first], func=RELU)
+        for start in (0, HALF // 2):
+            piece = slice(start, start + HALF // 2)
+            add_bias_layer1(0, start, HALF // 2)
+            nc.scalar.activation(out=result[:, piece], in_=summed[:, piece], func=RELU)
         nc.sync.dma_start(out=out_rows[:, first], in_=result[:, first])
-        add_bias_layer1(1)
+        add_bias_layer1(1, 0, HALF)
         nc.vector.tensor_scalar_max(out=result[:, second], in0=summed[:, second], scalar1=0.0)
         nc.sync.dma_start(out=out_rows[:, second], in_=result[:, second])

@@ -34,10 +34,10 @@ def regroup_layer0(nc, raw, grouped):
     nc.scalar.copy(out=target[:, :, :, PACK // 2 :], in_=source[:, :, :, PACK // 2 :])
 
 
-def regroup_layer1(copy, raw, grouped, cols):
-    source = raw[:].rearrange("p t (c i) -> p c t i", i=PACK)
-    target = grouped[:].rearrange("p (c i) t -> p c t i", i=PACK)
-    runs = slice(cols.start // PACK, cols.stop // PACK)
+def regroup_layer1(copy, raw, grouped, cols, run):
+    source = raw[:].rearrange("p t (c i) -> p c t i", i=run)
+    target = grouped[:].rearrange("p (c i) t -> p c t i", i=run)
+    runs = slice(cols.start // run, cols.stop // run)
     copy(out=target[:, runs], in_=source[:, runs])
 
 
@@ -181,10 +181,10 @@ def tile_can_s_kernel(tc, user_emb, item_emb, out):
             regroup_layer0(nc, raw[l, b], grouped[l, b])
 
         def vector_regroups(b, cols):
-            regroup_layer1(nc.vector.tensor_copy, raw[1, b], grouped[1, b], cols)
+            regroup_layer1(nc.vector.tensor_copy, raw[1, b], grouped[1, b], cols, 4)
 
         def scalar_regroups(b, cols):
-            regroup_layer1(nc.scalar.copy, raw[1, b], grouped[1, b], cols)
+            regroup_layer1(nc.scalar.copy, raw[1, b], grouped[1, b], cols, 8)
 
         def quantise_vectors_half(l, b):
             quantise_half(nc, grouped[l, b], codes[l, b], scales[l, b], HALVES[0])

@@ -28,10 +28,10 @@ FLOPS = 2 * SAMPLES * LAYERS * ROWS * D * D
 
 
 def regroup_layer0(nc, raw, grouped):
-    source = raw[:].rearrange("p t (m j) -> p m t j", j=PACK)
-    target = grouped[:].rearrange("p (j m) t -> p m t j", j=PACK)
-    nc.vector.tensor_copy(out=target[:, :, :, : PACK // 2], in_=source[:, :, :, : PACK // 2])
-    nc.scalar.copy(out=target[:, :, :, PACK // 2 :], in_=source[:, :, :, PACK // 2 :])
+    source = raw[:].rearrange("p t (c i j) -> p c t i j", i=2, j=PACK)
+    target = grouped[:].rearrange("p (j c i) t -> p c t i j", i=2, j=PACK)
+    nc.vector.tensor_copy(out=target[:, :, :, :, : PACK // 2], in_=source[:, :, :, :, : PACK // 2])
+    nc.scalar.copy(out=target[:, :, :, :, PACK // 2 :], in_=source[:, :, :, :, PACK // 2 :])
 
 
 def regroup_layer1(copy, raw, grouped, cols, run):
@@ -181,7 +181,7 @@ def tile_can_s_kernel(tc, user_emb, item_emb, out):
             regroup_layer0(nc, raw[l, b], grouped[l, b])
 
         def vector_regroups(b, cols):
-            regroup_layer1(nc.vector.tensor_copy, raw[1, b], grouped[1, b], cols, 4)
+            regroup_layer1(nc.vector.tensor_copy, raw[1, b], grouped[1, b], cols, 8)
 
         def scalar_regroups(b, cols):
             regroup_layer1(nc.scalar.copy, raw[1, b], grouped[1, b], cols, 8)

from contextlib import ExitStack

import concourse.mybir as mybir
from concourse.masks import make_identity

F32 = mybir.dt.float32
BF16 = mybir.dt.bfloat16
U32 = mybir.dt.uint32
U8 = mybir.dt.uint8
I32 = mybir.dt.int32
FP8X4 = mybir.dt.float8_e4m3fn_x4
ADD = mybir.AluOpType.add
RELU = mybir.ActivationFunctionType.Relu

P = 128
PACK = 4
D = P * PACK
HALF = D // 2
HALVES = (slice(0, HALF), slice(HALF, D))
VECTORS_COLUMNS = D // 4
BANK = 512
SAMPLES = 2
ROWS = 64
ALL_ROWS = SAMPLES * ROWS
LAYERS = 2

FLOPS = 2 * SAMPLES * LAYERS * ROWS * D * D


def regroup_layer0(nc, raw, grouped):
    source = raw[:].rearrange("p t (c i j) -> p c t i j", i=2, j=PACK)
    target = grouped[:].rearrange("p (j c i) t -> p c t i j", i=2, j=PACK)
    nc.vector.tensor_copy(out=target[:, :, :, :, : PACK // 2], in_=source[:, :, :, :, : PACK // 2])
    nc.scalar.copy(out=target[:, :, :, :, PACK // 2 :], in_=source[:, :, :, :, PACK // 2 :])


def regroup_layer1(copy, raw, grouped, cols, run):
    source = raw[:].rearrange("p t (c i) -> p c t i", i=run)
    target = grouped[:].rearrange("p (c i) t -> p c t i", i=run)
    runs = slice(cols.start // run, cols.stop // run)
    copy(out=target[:, runs], in_=source[:, runs])


def quantise_half(nc, grouped, codes, scales, cols):
    nc.vector.quantize_mx(
        out=codes[:, cols].bitcast(FP8X4),
        scales=scales[:, cols],
        in_=grouped[:, cols, :].rearrange("p c t -> p (c t)"),
    )


def tile_can_s_kernel(tc, user_emb, item_emb, out):
    nc = tc.nc
    params = item_emb.rearrange("b (l r) -> (b l) r", l=LAYERS)
    out_rows = out.rearrange("b n e -> (b n) e")

    with ExitStack() as ctx:
        keep = ctx.enter_context(tc.tile_pool(name="keep", bufs=1))
        psum = ctx.enter_context(tc.psum_pool(name="psum", bufs=1))
        ctx.enter_context(tc.manual_schedule())

        x_rows = keep.tile([ALL_ROWS, D], BF16)
        nc.sync.dma_start(out=x_rows[:], in_=user_emb.rearrange("b n k -> (b n) k"))
        bias = keep.tile([P, SAMPLES, LAYERS, PACK], BF16)
        nc.sync.dma_start(
            out=bias[:].rearrange("m b l j -> m (b l) j"),
            in_=params[:, D * D :].rearrange("q (m j) -> m q j", j=PACK),
        )
        raw, grouped, codes, scales = {}, {}, {}, {}
        for l in range(LAYERS):
            for b in range(SAMPLES):
                tail = "%d%d" % (l, b)
                raw[l, b] = keep.tile([P, PACK, D], BF16, name="raw" + tail)
                nc.sync.dma_start(
                    out=raw[l, b][:],
                    in_=params[LAYERS * b + l, : D * D].rearrange("(p t e) -> p t e", t=PACK, e=D),
                )
                grouped[l, b] = keep.tile([P, D, PACK], BF16, name="grouped" + tail, align_bytes=64)
                codes[l, b] = keep.tile([P, D], U32, name="codes" + tail, align_bytes=64)
                scales[l, b] = keep.tile([P, D], U8, name="scales" + tail, align_bytes=64)

        ident = keep.tile([P, P], F32)
        make_identity(nc, ident[:])
        ident_bf16 = keep.tile([P, P], BF16)
        make_identity(nc, ident_bf16[:])

        h_codes = keep.tile([P, SAMPLES * ALL_ROWS], U32, align_bytes=64)
        h_scales = keep.tile([P, SAMPLES * ALL_ROWS], U8, align_bytes=64)
        nc.vector.memset(h_codes[:].bitcast(I32), 0)
        nc.vector.memset(h_scales[:].bitcast(I32), 0)
        h_sum = keep.tile([P, SAMPLES, ROWS, PACK], BF16, align_bytes=64)
        h_grouped = keep.tile([P, SAMPLES, ROWS, PACK], BF16, align_bytes=64)

        bias_cols = keep.tile([P, PACK, ALL_ROWS], BF16)

        nc.vector.tensor_copy(
            out=bias_cols[:].rearrange("m j (b n) -> m j b n", b=SAMPLES),
            in_=bias[:, :, 1, :].rearrange("m b j -> m j b").unsqueeze(3).to_broadcast([P, PACK, SAMPLES, ROWS]),
        )

        x_words = x_rows[:].bitcast(F32).rearrange("r (p u) -> r u p", u=2)
        x_t = psum.tile([P, 2, ALL_ROWS], F32)
        for u in range(2):
            nc.tensor.transpose(x_t[:, u, :], x_words[:, u, :], ident[:])
        x_grouped = keep.tile([P, ALL_ROWS * PACK], BF16, align_bytes=64)
        nc.vector.tensor_copy(
            out=x_grouped[:].bitcast(F32).rearrange("p (r u) -> p r u", u=2),
            in_=x_t[:].rearrange("p u r -> p r u"),
        )
        x_codes = keep.tile([P, ALL_ROWS], U32, align_bytes=64)
        x_scales = keep.tile([P, ALL_ROWS], U8, align_bytes=64)
        nc.vector.quantize_mx(out=x_codes[:].bitcast(FP8X4), scales=x_scales[:], in_=x_grouped[:])

        bias_t = psum.tile([ALL_ROWS, PACK, P], BF16)
        for j in range(PACK):
            nc.tensor.transpose(bias_t[:, j, :], bias_cols[:, j, :], ident_bf16[:])
        bias_rows = keep.tile([ALL_ROWS, PACK, P], BF16)

        h_t = {}
        for b in range(SAMPLES):
            h_t[b] = psum.tile([P, PACK, ALL_ROWS], F32, name="h_t%d" % b)

        def multiply_layer0(b):
            for j in range(PACK):
                block = slice(j * P, (j + 1) * P)
                nc.tensor.matmul_mx(
                    out=h_t[b][:, j, :],
                    lhsT=codes[0, b][:, block].bitcast(FP8X4),
                    lhsT_scale=scales[0, b][:, block],
                    rhs=x_codes[:].bitcast(FP8X4),
                    rhs_scale=x_scales[:],
                    start=True,
                    stop=True,
                )

        def add_bias_layer0(b):
            own = slice(b * ROWS, (b + 1) * ROWS)
            nc.vector.tensor_tensor(
                out=h_sum[:, SAMPLES - 1 - b, :, :],
                in0=h_t[b][:, :, own].rearrange("p j n -> p n j"),
                in1=bias[:, b, 0, :].unsqueeze(1).to_broadcast([P, ROWS, PACK]),
                op=ADD,
            )

        def relu_layer0():
            nc.vector.tensor_scalar_max(
                out=h_grouped[:].rearrange("p b n j -> p (b n j)"),
                in0=h_sum[:].rearrange("p b n j -> p (b n j)"),
                scalar1=0.0,
            )

        product = [psum.tile([ALL_ROWS, BANK], F32, name="product%d" % c) for c in range(len(HALVES))]

        def multiply_layer1(b, c):
            cols = HALVES[c]
            rows = slice((SAMPLES - 1 - b) * ALL_ROWS, (SAMPLES - b) * ALL_ROWS)
            nc.tensor.matmul_mx(
                out=product[c][:, :HALF],
                lhsT=h_codes[:, rows].bitcast(FP8X4),
                lhsT_scale=h_scales[:, rows],
                rhs=codes[1, b][:, cols].bitcast(FP8X4),
                rhs_scale=scales[1, b][:, cols],
                start=(b == 0),
                stop=(b == SAMPLES - 1),
            )

        idle_bank = psum.tile([ALL_ROWS, BANK], F32)

        def keep_tensor_engine_busy(b):
            nc.tensor.matmul_mx(
                out=idle_bank[:],
                lhsT=x_codes[:].bitcast(FP8X4),
                lhsT_scale=x_scales[:],
                rhs=codes[0, b][:].bitcast(FP8X4),
                rhs_scale=scales[0, b][:],
                start=True,
                stop=True,
            )

        def regroup(l, b):
            regroup_layer0(nc, raw[l, b], grouped[l, b])

        def vector_regroups(b, cols):
            regroup_layer1(nc.vector.tensor_copy, raw[1, b], grouped[1, b], cols, 8)

        def scalar_regroups(b, cols):
            regroup_layer1(nc.scalar.copy, raw[1, b], grouped[1, b], cols, 8)

        def quantise_vectors_half(l, b):
            quantise_half(nc, grouped[l, b], codes[l, b], scales[l, b], HALVES[0])

        def quantise_scalars_half(l, b):
            quantise_half(nc, grouped[l, b], codes[l, b], scales[l, b], HALVES[1])

        regroup(0, 0)
        nc.vector.tensor_copy(out=bias_rows[:], in_=bias_t[:])
        quantise_vectors_half(0, 0)
        regroup(0, 1)
        quantise_scalars_half(0, 0)
        multiply_layer0(0)
        quantise_vectors_half(0, 1)
        quantise_scalars_half(0, 1)
        multiply_layer0(1)
        for b in (0, 1, 0, 1):
            keep_tensor_engine_busy(b)
        vector_regroups(0, slice(0, VECTORS_COLUMNS))
        scalar_regroups(0, slice(VECTORS_COLUMNS, HALF))
        scalar_regroups(0, HALVES[1])
        add_bias_layer0(0)
        quantise_vectors_half(1, 0)
        add_bias_layer0(1)
        vector_regroups(1, slice(0, HALF - D // 8))
        scalar_regroups(1, slice(HALF - D // 8, HALF))
        scalar_regroups(1, HALVES[1])
        relu_layer0()
        quantise_scalars_half(1, 0)
        live = slice(ROWS, ROWS + ALL_ROWS)
        nc.vector.quantize_mx(
            out=h_codes[:, live].bitcast(FP8X4),
            scales=h_scales[:, live],
            in_=h_grouped[:].rearrange("p b n j -> p (b n j)"),
        )
        multiply_layer1(0, 0)
        multiply_layer1(0, 1)
        quantise_vectors_half(1, 1)
        multiply_layer1(1, 0)
        quantise_scalars_half(1, 1)
        multiply_layer1(1, 1)

        first, second = HALVES
        summed = keep.tile([ALL_ROWS, D], F32)
        result = keep.tile([ALL_ROWS, D], F32)

        def add_bias_layer1(c, start, width):
            cols = slice(c * HALF + start, c * HALF + start + width)
            nc.vector.tensor_tensor(
                out=summed[:, cols].rearrange("r (m j) -> r m j", j=PACK),
                in0=product[c][:, start : start + width].rearrange("r (m j) -> r m j", j=PACK),
                in1=bias_rows[:, :, cols.start // PACK : cols.stop // PACK].rearrange("r j m -> r m j"),
                op=ADD,
            )

        for start in (0, HALF // 2):
            piece = slice(start, start + HALF // 2)
            add_bias_layer1(0, start, HALF // 2)
            nc.scalar.activation(out=result[:, piece], in_=summed[:, piece], func=RELU)
        nc.sync.dma_start(out=out_rows[:, first], in_=result[:, first])
        add_bias_layer1(1, 0, HALF)
        nc.vector.tensor_scalar_max(out=result[:, second], in0=summed[:, second], scalar1=0.0)
        nc.sync.dma_start(out=out_rows[:, second], in_=result[:, second])
